import numpy as np
import ml_dtypes


def mxq(x, axis, fmt="e4m3"):
    dtype, down = {"e4m3": (ml_dtypes.float8_e4m3fn, 7), "e5m2": (ml_dtypes.float8_e5m2, 14)}[fmt]
    v = np.moveaxis(np.asarray(x, np.float32).astype(ml_dtypes.bfloat16).astype(np.float64), axis, -1)
    blocks = v.reshape(v.shape[:-1] + (-1, 32))
    amax = np.abs(blocks).max(-1, keepdims=True)
    byte = np.maximum(np.where(amax > 0, np.frexp(amax)[1] - 1 + 127, 0) - down, 1)
    scale = np.exp2(byte - 127.0)
    codes = (blocks / scale).astype(np.float32).astype(dtype).astype(np.float64)
    return np.moveaxis((codes * scale).reshape(v.shape), -1, axis)


WIDE = False


def mx_kscale(k):
    if not WIDE:
        return np.ones(k)
    levels = np.array([10, -10, 5, -5, 0])
    a = np.random.permutation(np.resize(levels, k // 512 * 4)).reshape(k // 512, 4)
    idx = np.arange(k)
    return np.exp2(a[idx // 512, idx % 128 // 32])


BF16 = ml_dtypes.bfloat16


def bf(x):
    return np.asarray(x, np.float32).astype(BF16)


def f64(x):
    return np.asarray(x).astype(np.float64)


B, T, D, O = 128, 32, 512, 512


def erf(z):
    a = np.clip(z, -6.0, 6.0)
    q = 2.0 * a * a
    term = a.copy()
    total = a.copy()
    for k in range(1, 130):
        term = term * q / (2 * k + 1)
        total = total + term
    return 2.0 / np.sqrt(np.pi) * np.exp(-a * a) * total


def gelu_exact(v):
    return 0.5 * v * (1.0 + erf(v / np.sqrt(2.0)))


def setup_inputs():
    s = mx_kscale(D)
    x = np.random.standard_normal((B, T, D)) * s
    lengths = np.random.randint(T // 4, T + 1, size=B)
    lengths[np.random.randint(B)] = T
    pad = np.arange(T)[None, :] >= lengths[:, None]
    x = np.where(pad[:, :, None], -1.0, x)
    return {"x": bf(x), "W": bf(np.random.standard_normal((O, D)) / np.sqrt(D) / s[None, :]), "b": bf(np.random.standard_normal(O) * 0.3)}


def reference(x, W, b):
    x = f64(x)
    valid = ~np.all(x == -1.0, axis=-1)
    y = gelu_exact((mxq(x, 2, "e4m3") @ mxq(f64(W), 1, "e4m3").T) + f64(b))
    vf = valid[..., None].astype(np.float64)
    n = np.sum(vf, axis=1)
    mean = np.sum(y * vf, axis=1) / n
    diff = (y - mean[:, None, :]) * vf
    var = np.sum(diff * diff, axis=1) / np.maximum(n - 1.0, 1.0)
    std = np.where(n > 1.0, np.sqrt(var), np.zeros_like(var))
    out = np.concatenate([std, mean], axis=-1)
    return np.where(np.isnan(out), np.zeros_like(out), out)

@@ -1,0 +1,345 @@
+from contextlib import ExitStack
+
+import concourse.mybir as mybir
+from concourse.masks import make_identity
+
+FP8X4 = mybir.dt.float8_e4m3fn_x4
+F32 = mybir.dt.float32
+BF16 = mybir.dt.bfloat16
+U32 = mybir.dt.uint32
+U8 = mybir.dt.uint8
+ACT = mybir.ActivationFunctionType
+ALU = mybir.AluOpType
+AX = mybir.AxisListType
+
+P = 128
+SAMPLES, TOKENS, K, OUT = 128, 32, 512, 512
+GROUPS = 8
+SLOTS = 4
+OB = OUT // P
+FLOPS = 2 * SAMPLES * TOKENS * K * OUT
+PAD_WORD = -(1.0 + 0xBF80 / 2.0**23)
+
+FIRST = [0, 1, 2]
+LAST = 3
+
+
+def tile_linearnnencoder_kernel(tc, x, W, b, out):
+    nc = tc.nc
+    with ExitStack() as ctx:
+        const = ctx.enter_context(tc.tile_pool(name="const", bufs=1))
+        xpool = ctx.enter_context(tc.tile_pool(name="xpool", bufs=GROUPS))
+        gpool = ctx.enter_context(tc.tile_pool(name="gpool", bufs=2))
+        cpool = ctx.enter_context(tc.tile_pool(name="cpool", bufs=GROUPS + 1))
+        mpool = ctx.enter_context(tc.tile_pool(name="mpool", bufs=3))
+        jpool = ctx.enter_context(tc.tile_pool(name="jpool", bufs=2))
+        ypool = ctx.enter_context(tc.tile_pool(name="ypool", bufs=6))
+        fpool = ctx.enter_context(tc.tile_pool(name="fpool", bufs=2))
+        psum_t = ctx.enter_context(tc.psum_pool(name="psum_t", bufs=3))
+        psum_a = ctx.enter_context(tc.psum_pool(name="psum_a", bufs=4))
+        psum_s = ctx.enter_context(tc.psum_pool(name="psum_s", bufs=1))
+        ctx.enter_context(tc.manual_schedule())
+
+        b_rows = const.tile([P, P], BF16, name="b_rows")
+        nc.vector.memset(b_rows[:], 0.0)
+        nc.scalar.dma_start(out=b_rows[0:OB, :], in_=b.rearrange("(ob o) -> ob o", ob=OB))
+        x_groups = x.flatten_outer_dims().rearrange("(g p e) k -> g p (e k)", g=GROUPS, p=P, e=SLOTS)
+        x_sb = []
+        w_sb = const.tile([P, SLOTS * K], BF16, name="w_sb")
+        for g in range(GROUPS):
+            xin = xpool.tile([P, SLOTS * K], BF16, name="xin", tag="xin")
+            nc.sync.dma_start(out=xin[:], in_=x_groups[g])
+            x_sb.append(xin)
+            if g == 0:
+                nc.sync.dma_start(
+                    out=w_sb[:].rearrange("p (ob k) -> p ob k", ob=OB),
+                    in_=W.rearrange("(ob p) k -> p ob k", p=P),
+                )
+
+        ident = const.tile([P, P], F32, name="ident")
+        make_identity(nc, ident[:])
+        ones_f = const.tile([P, 1], F32, name="ones_f")
+        nc.vector.memset(ones_f[:], 1.0)
+        warm = const.tile([P, 1], F32, name="warm")
+        nc.scalar.activation(out=warm[:], in_=ones_f[:], func=ACT.Gelu)
+        neg_pad = const.tile([P, 1], F32, name="neg_pad")
+        nc.vector.memset(neg_pad[:], -PAD_WORD)
+        ones_bf = const.tile([P, 2], BF16, name="ones_bf")
+        nc.vector.memset(ones_bf[:], 1.0)
+        ident_bf = const.tile([P, OB], BF16, name="ident_bf")
+        nc.vector.tensor_copy(out=ident_bf[:], in_=ident[:, 0:OB])
+        group_of = const.tile([P, 16], F32, name="group_of")
+        nc.vector.tensor_reduce(
+            out=group_of[:], in_=ident[:].rearrange("p (s q) -> p s q", q=8), axis=AX.X, op=ALU.add
+        )
+
+        stats = const.tile([P, OB, SAMPLES, 3], F32, name="stats")
+        res = const.tile([P, 2 * OUT], F32, name="res")
+        var = const.tile([P, OUT], F32, name="var")
+        dist = const.tile([P, GROUPS * SLOTS], F32, name="dist")
+
+        def pad_test(g, slots):
+            words = x_sb[g][:].bitcast(F32)
+            for e in slots:
+                junk = jpool.tile([P, 256], BF16, name="junk", tag="junk")
+                col = SLOTS * g + e
+                nc.scalar.activation(
+                    out=junk[:],
+                    in_=words[:, e * 256 : (e + 1) * 256],
+                    func=ACT.Square,
+                    bias=neg_pad[:, 0:1],
+                    scale=1.0,
+                    accum_out=dist[:, col : col + 1],
+                )
+
+        def masked_identities(g):
+            mid = mpool.tile([P, SLOTS, P], F32, name="mid", tag="mid")
+            for e in range(SLOTS):
+                col = SLOTS * g + e
+                nc.vector.tensor_scalar(
+                    out=mid[:, e, :], in0=ident[:], scalar1=dist[:, col : col + 1], scalar2=0.0,
+                    op0=ALU.mult, op1=ALU.is_gt,
+                )
+            return [mid[:, e, :] for e in range(SLOTS)]
+
+        def transposes(src, idents):
+            words = src[:].bitcast(F32)
+            halves = []
+            for h in range(2):
+                xt = psum_t.tile([P, 2, 2, P], F32, name="xt", tag="xt")
+                for e2 in range(2):
+                    for u in range(2):
+                        c0 = (2 * h + e2) * 256 + u * P
+                        nc.tensor.transpose(xt[:, e2, u, :], words[:, c0 : c0 + P], idents[2 * h + e2])
+                halves.append(xt)
+            return halves
+
+        def new_grouped():
+            return gpool.tile([P, SLOTS * K], BF16, name="grouped", tag="grouped", align_bytes=64)
+
+        def regroup(grouped, halves, h, engine):
+            dst = grouped[:].bitcast(F32)[:, h * 512 : (h + 1) * 512].rearrange("k (e p u) -> k e p u", e=2, p=P, u=2)
+            src = halves[h][:].rearrange("k e u p -> k e p u")
+            if engine == "scalar":
+                nc.scalar.copy(out=dst, in_=src)
+            else:
+                nc.vector.tensor_copy(out=dst, in_=src)
+
+        def quantise(grouped):
+            codes = cpool.tile([P, 512], U32, name="codes", tag="codes", align_bytes=64)
+            scales = cpool.tile([P, 512], U8, name="scales", tag="scales", align_bytes=64)
+            nc.vector.quantize_mx(out=codes[:].bitcast(FP8X4), scales=scales[:], in_=grouped[:])
+            return codes, scales
+
+        def mx_pass(g, ob):
+            acc = psum_a.tile([P, 512], F32, name="acc", tag="acc")
+            nc.tensor.matmul_mx(
+                out=acc[:],
+                lhsT=w_codes[:, ob * P : (ob + 1) * P].bitcast(FP8X4),
+                lhsT_scale=w_scales[:, ob * P : (ob + 1) * P],
+                rhs=x_q[g][0][:].bitcast(FP8X4),
+                rhs_scale=x_q[g][1][:],
+                start=True,
+                stop=True,
+            )
+            return acc
+
+        def gelu(acc, ob):
+            y = ypool.tile([P, 512], F32, name="y", tag="y")
+            nc.scalar.activation(out=y[:], in_=acc[:], func=ACT.Gelu, bias=b_col[:, ob : ob + 1], scale=1.0)
+            return y
+
+        def statistics(g, ob, y):
+            yv = y[:].rearrange("o (e j r q) -> o j e q r", e=SLOTS, j=8, r=2, q=8)
+            for j in range(8):
+                s0 = 16 * g + 2 * j
+                nc.vector.bn_stats(
+                    out=stats[:, ob, s0 : s0 + 2, :].rearrange("o s c -> o (s c)"), in_=yv[:, j]
+                )
+
+        def to_sample_rows(blocks):
+            mean_t = psum_t.tile([P, 512], F32, name="mean_t", tag="xt")
+            m2_t = psum_t.tile([P, 512], F32, name="m2_t", tag="xt")
+            for i, ob in enumerate(blocks):
+                nc.tensor.transpose(mean_t[:, i * P : (i + 1) * P], stats[:, ob, :, 1], ident[:])
+            for i, ob in enumerate(blocks):
+                nc.tensor.transpose(m2_t[:, i * P : (i + 1) * P], stats[:, ob, :, 2], ident[:])
+            return mean_t, m2_t
+
+        mids = {}
+        halves = {}
+        grouped = {}
+        x_q = {}
+        accs = {}
+        pad_test(0, range(SLOTS))
+        mids[0] = masked_identities(0)
+        w_halves = transposes(w_sb, [ident[:]] * SLOTS)
+        b_ps = psum_s.tile([P, OB], F32, name="b_ps", tag="misc")
+        nc.tensor.matmul(out=b_ps[:], lhsT=b_rows[:], rhs=ident_bf[:], start=True, stop=True)
+        w_grouped = new_grouped()
+        regroup(w_grouped, w_halves, 0, "scalar")
+        regroup(w_grouped, w_halves, 1, "vector")
+        halves[0] = transposes(x_sb[0], mids[0])
+        w_codes, w_scales = quantise(w_grouped)
+        b_col = const.tile([P, OB], F32, name="b_col")
+        nc.vector.tensor_copy(out=b_col[:], in_=b_ps[:])
+        grouped[0] = new_grouped()
+        regroup(grouped[0], halves[0], 0, "scalar")
+        regroup(grouped[0], halves[0], 1, "vector")
+        pad_test(1, range(SLOTS))
+        x_q[0] = quantise(grouped[0])
+        mids[1] = masked_identities(1)
+        for ob in FIRST:
+            accs[0, ob] = mx_pass(0, ob)
+        halves[1] = transposes(x_sb[1], mids[1])
+        pad_test(2, [0, 1])
+
+        for g in range(GROUPS):
+            y0 = gelu(accs[g, FIRST[0]], FIRST[0])
+            if g == 0:
+                pad_test(2, [2, 3])
+            if g + 1 < GROUPS:
+                grouped[g + 1] = new_grouped()
+                regroup(grouped[g + 1], halves[g + 1], 0, "scalar")
+                regroup(grouped[g + 1], halves[g + 1], 1, "vector")
+            statistics(g, FIRST[0], y0)
+            if g + 1 < GROUPS:
+                x_q[g + 1] = quantise(grouped[g + 1])
+            if g + 2 < GROUPS:
+                mids[g + 2] = masked_identities(g + 2)
+            if g + 1 < GROUPS:
+                for ob in FIRST:
+                    accs[g + 1, ob] = mx_pass(g + 1, ob)
+            else:
+                accs[0, LAST] = mx_pass(0, LAST)
+            if g + 2 < GROUPS:
+                halves[g + 2] = transposes(x_sb[g + 2], mids[g + 2])
+            y1 = gelu(accs[g, FIRST[1]], FIRST[1])
+            if g + 3 < GROUPS:
+                pad_test(g + 3, [0, 1])
+            statistics(g, FIRST[1], y1)
+            y2 = gelu(accs[g, FIRST[2]], FIRST[2])
+            if g + 3 < GROUPS:
+                pad_test(g + 3, [2, 3])
+            if g == GROUPS - 2:
+                valid = const.tile([P, GROUPS * SLOTS], F32, name="valid")
+                nc.vector.tensor_scalar(out=valid[:], in0=dist[:], scalar1=0.0, scalar2=None, op0=ALU.is_gt)
+                valid4 = const.tile([P, GROUPS], F32, name="valid4")
+                nc.vector.tensor_reduce(
+                    out=valid4[:], in_=valid[:].rearrange("p (g e) -> p g e", e=SLOTS), axis=AX.X, op=ALU.add
+                )
+                spread = const.tile([P, GROUPS, 16], BF16, name="spread")
+                nc.vector.tensor_tensor(
+                    out=spread[:],
+                    in0=valid4[:].unsqueeze(2).to_broadcast([P, GROUPS, 16]),
+                    in1=group_of[:].unsqueeze(1).to_broadcast([P, GROUPS, 16]),
+                    op=ALU.mult,
+                )
+                nv_ps = psum_s.tile([P, 1], F32, name="nv_ps", tag="misc")
+                nc.tensor.matmul(
+                    out=nv_ps[:], lhsT=spread[:].rearrange("p g s -> p (g s)"), rhs=ones_bf[:, 0:1],
+                    start=True, stop=True,
+                )
+            statistics(g, FIRST[2], y2)
+
+        nval = const.tile([P, 1], F32, name="nval")
+        nc.vector.tensor_copy(out=nval[:], in_=nv_ps[:])
+        npad = const.tile([P, 1], F32, name="npad")
+        nc.vector.tensor_scalar(
+            out=npad[:], in0=nval[:], scalar1=-1.0, scalar2=float(TOKENS), op0=ALU.mult, op1=ALU.add
+        )
+        nmax = const.tile([P, 1], F32, name="nmax")
+        nc.vector.tensor_scalar_max(out=nmax[:], in0=nval[:], scalar1=1.0)
+        rn = const.tile([P, 1], F32, name="rn")
+        nc.vector.reciprocal(out=rn[:], in_=nmax[:])
+        nz = const.tile([P, 1], F32, name="nz")
+        nc.vector.tensor_scalar_min(out=nz[:], in0=nval[:], scalar1=1.0)
+        a2 = const.tile([P, 1], F32, name="a2")
+        nc.vector.tensor_scalar(
+            out=a2[:], in0=rn[:], scalar1=nz[:, 0:1], scalar2=float(TOKENS), op0=ALU.mult, op1=ALU.mult
+        )
+        rneg = const.tile([P, 1], F32, name="rneg")
+        nc.vector.tensor_scalar(
+            out=rneg[:], in0=npad[:], scalar1=rn[:, 0:1], scalar2=-float(TOKENS), op0=ALU.mult, op1=ALU.mult
+        )
+        n1 = const.tile([P, 1], F32, name="n1")
+        nc.vector.tensor_scalar(out=n1[:], in0=nval[:], scalar1=-1.0, scalar2=1.0, op0=ALU.add, op1=ALU.max)
+        rn1 = const.tile([P, 1], F32, name="rn1")
+        nc.vector.reciprocal(out=rn1[:], in_=n1[:])
+        cinv = const.tile([P, 1], F32, name="cinv")
+        nc.vector.tensor_scalar(
+            out=cinv[:], in0=nval[:], scalar1=1.0, scalar2=rn1[:, 0:1], op0=ALU.is_gt, op1=ALU.mult
+        )
+
+        for g in (1, 2, 3):
+            accs[g, LAST] = mx_pass(g, LAST)
+        y = gelu(accs[0, LAST], LAST)
+        ypad = const.tile([P, OB], F32, name="ypad")
+        nc.scalar.activation(out=ypad[:], in_=b_col[:], func=ACT.Gelu)
+        statistics(0, LAST, y)
+        ypad_bc = psum_t.tile([P, OUT], F32, name="ypad_bc", tag="xt")
+        for ob in range(OB):
+            nc.tensor.matmul(
+                out=ypad_bc[:, ob * P : (ob + 1) * P],
+                lhsT=ypad[:, ob : ob + 1].to_broadcast([P, P]),
+                rhs=ident[:],
+                start=True,
+                stop=True,
+            )
+        statistics(1, LAST, gelu(accs[1, LAST], LAST))
+        ypad_nz = const.tile([P, OUT], F32, name="ypad_nz")
+        nc.vector.tensor_scalar(out=ypad_nz[:], in0=ypad_bc[:], scalar1=nz[:, 0:1], scalar2=None, op0=ALU.mult)
+        accs[4, LAST] = mx_pass(4, LAST)
+        statistics(2, LAST, gelu(accs[2, LAST], LAST))
+
+        nf = len(FIRST) * P
+        mean_t, m2_t = to_sample_rows(FIRST)
+        accs[5, LAST] = mx_pass(5, LAST)
+        d = fpool.tile([P, 512], F32, name="d", tag="d")
+        nc.vector.tensor_tensor(out=d[:, :nf], in0=mean_t[:, :nf], in1=ypad_nz[:, :nf], op=ALU.subtract)
+        nc.vector.scalar_tensor_tensor(
+            out=res[:, OUT : OUT + nf], in0=d[:, :nf], scalar=a2[:, 0:1], in1=ypad_nz[:, :nf], op0=ALU.mult, op1=ALU.add
+        )
+        nc.sync.dma_start(out=out[:, OUT : OUT + nf], in_=res[:, OUT : OUT + nf])
+        y3 = gelu(accs[3, LAST], LAST)
+        dd = fpool.tile([P, 512], F32, name="dd", tag="dd")
+        nc.scalar.activation(out=dd[:, :nf], in_=d[:, :nf], func=ACT.Square)
+        statistics(3, LAST, y3)
+        m2v = fpool.tile([P, 512], F32, name="m2v", tag="m2v")
+        nc.vector.scalar_tensor_tensor(
+            out=m2v[:, :nf], in0=dd[:, :nf], scalar=rneg[:, 0:1], in1=m2_t[:, :nf], op0=ALU.mult, op1=ALU.add
+        )
+        accs[6, LAST] = mx_pass(6, LAST)
+        statistics(4, LAST, gelu(accs[4, LAST], LAST))
+        accs[7, LAST] = mx_pass(7, LAST)
+        statistics(5, LAST, gelu(accs[5, LAST], LAST))
+        nc.scalar.activation(out=var[:, :nf], in_=m2v[:, :nf], func=ACT.Relu, scale=cinv[:, 0:1])
+        statistics(6, LAST, gelu(accs[6, LAST], LAST))
+        statistics(7, LAST, gelu(accs[7, LAST], LAST))
+
+        warm2 = const.tile([P, 1], F32, name="warm2")
+        nc.scalar.activation(out=warm2[:], in_=ones_f[:], func=ACT.Sqrt)
+        nc.scalar.activation(out=res[:, :nf], in_=var[:, :nf], func=ACT.Sqrt)
+        nc.sync.dma_start(out=out[:, :nf], in_=res[:, :nf])
+        c0 = LAST * P
+        mean_l, m2_l = to_sample_rows([LAST])
+        dl = fpool.tile([P, 512], F32, name="dl", tag="d")
+        nc.vector.tensor_tensor(out=dl[:, :P], in0=mean_l[:, :P], in1=ypad_nz[:, c0 : c0 + P], op=ALU.subtract)
+        ddl = fpool.tile([P, 512], F32, name="ddl", tag="dd")
+        nc.vector.scalar_tensor_tensor(
+            out=ddl[:, :P], in0=dl[:, :P], scalar=rneg[:, 0:1], in1=dl[:, :P], op0=ALU.mult, op1=ALU.mult
+        )
+        m2l = fpool.tile([P, 512], F32, name="m2l", tag="m2v")
+        nc.vector.tensor_tensor(out=m2l[:, :P], in0=m2_l[:, :P], in1=ddl[:, :P], op=ALU.add)
+        nc.scalar.activation(out=var[:, c0 : c0 + P], in_=m2l[:, :P], func=ACT.Relu, scale=cinv[:, 0:1])
+        nc.vector.scalar_tensor_tensor(
+            out=res[:, OUT + c0 : OUT + c0 + P],
+            in0=dl[:, :P],
+            scalar=a2[:, 0:1],
+            in1=ypad_nz[:, c0 : c0 + P],
+            op0=ALU.mult,
+            op1=ALU.add,
+        )
+        nc.sync.dma_start(out=out[:, OUT + c0 : OUT + c0 + P], in_=res[:, OUT + c0 : OUT + c0 + P])
+        nc.scalar.activation(out=res[:, c0 : c0 + P], in_=var[:, c0 : c0 + P], func=ACT.Sqrt)
+        nc.sync.dma_start(out=out[:, c0 : c0 + P], in_=res[:, c0 : c0 + P])

@@ -38,7 +38,6 @@ def tile_linearnnencoder_kernel(tc, x, W, b, out):
         psum_t = ctx.enter_context(tc.psum_pool(name="psum_t", bufs=3))
         psum_a = ctx.enter_context(tc.psum_pool(name="psum_a", bufs=4))
         psum_s = ctx.enter_context(tc.psum_pool(name="psum_s", bufs=1))
-        ctx.enter_context(tc.manual_schedule())
 
         b_rows = const.tile([P, P], BF16, name="b_rows")
         nc.vector.memset(b_rows[:], 0.0)
@@ -318,9 +317,7 @@ def tile_linearnnencoder_kernel(tc, x, W, b, out):
         statistics(7, LAST, gelu(accs[7, LAST], LAST))
 
         warm2 = const.tile([P, 1], F32, name="warm2")
-        nc.scalar.activation(out=warm2[:], in_=ones_f[:], func=ACT.Sqrt)
-        nc.scalar.activation(out=res[:, :nf], in_=var[:, :nf], func=ACT.Sqrt)
-        nc.sync.dma_start(out=out[:, :nf], in_=res[:, :nf])
+        nc.scalar.activation(out=warm2[:], in_=stats[:, LAST, 16 * (GROUPS - 1), 0:1], func=ACT.Sqrt)
         c0 = LAST * P
         mean_l, m2_l = to_sample_rows([LAST])
         dl = fpool.tile([P, 512], F32, name="dl", tag="d")
@@ -341,5 +338,5 @@ def tile_linearnnencoder_kernel(tc, x, W, b, out):
             op1=ALU.add,
         )
         nc.sync.dma_start(out=out[:, OUT + c0 : OUT + c0 + P], in_=res[:, OUT + c0 : OUT + c0 + P])
-        nc.scalar.activation(out=res[:, c0 : c0 + P], in_=var[:, c0 : c0 + P], func=ACT.Sqrt)
-        nc.sync.dma_start(out=out[:, c0 : c0 + P], in_=res[:, c0 : c0 + P])
+        nc.scalar.activation(out=res[:, :OUT], in_=var[:], func=ACT.Sqrt)
+        nc.sync.dma_start(out=out[:, :OUT], in_=res[:, :OUT])

@@ -119,7 +119,7 @@ def tile_linearnnencoder_kernel(tc, x, W, b, out):
         def regroup(grouped, halves, h, engine):
             dst = grouped[:].bitcast(F32)[:, h * 512 : (h + 1) * 512].rearrange("k (e p u) -> k e p u", e=2, p=P, u=2)
             src = halves[h][:].rearrange("k e u p -> k e p u")
-            if engine == "scalar":
+            if engine in ("scalar", "vector"):
                 nc.scalar.copy(out=dst, in_=src)
             else:
                 nc.vector.tensor_copy(out=dst, in_=src)

@@ -22,6 +22,7 @@ PAD_WORD = -(1.0 + 0xBF80 / 2.0**23)
 
 FIRST = [0, 1, 2]
 LAST = 3
+V_TEST = (1, 2, 3)
 
 
 def tile_linearnnencoder_kernel(tc, x, W, b, out):
@@ -75,28 +76,43 @@ def tile_linearnnencoder_kernel(tc, x, W, b, out):
         stats = const.tile([P, OB, SAMPLES, 3], F32, name="stats")
         res = const.tile([P, 2 * OUT], F32, name="res")
         var = const.tile([P, OUT], F32, name="var")
-        dist = const.tile([P, GROUPS * SLOTS], F32, name="dist")
+        dist = const.tile([P, GROUPS, 8], F32, name="dist")
+        perm = const.tile([P, P], F32, name="perm")
+        nc.vector.tensor_copy(
+            out=perm[:].rearrange("p (j q r) -> p j q r", j=8, q=8, r=2),
+            in_=ident[:].rearrange("p (j r q) -> p j q r", j=8, r=2, q=8),
+        )
 
         def pad_test(g, slots):
             words = x_sb[g][:].bitcast(F32)
             for e in slots:
-                junk = jpool.tile([P, 256], BF16, name="junk", tag="junk")
-                col = SLOTS * g + e
-                nc.scalar.activation(
-                    out=junk[:],
-                    in_=words[:, e * 256 : (e + 1) * 256],
-                    func=ACT.Square,
-                    bias=neg_pad[:, 0:1],
-                    scale=1.0,
-                    accum_out=dist[:, col : col + 1],
-                )
+                if g in V_TEST:
+                    junkv = jpool.tile([P, 256], BF16, name="junkv", tag="junkv")
+                    nc.vector.tensor_scalar(
+                        out=junkv[:],
+                        in0=words[:, e * 256 : (e + 1) * 256],
+                        scalar1=PAD_WORD,
+                        scalar2=None,
+                        op0=ALU.not_equal,
+                        op1=ALU.add,
+                        accum_out=dist[:, g, e : e + 1],
+                    )
+                else:
+                    junk = jpool.tile([P, 256], BF16, name="junk", tag="junk")
+                    nc.scalar.activation(
+                        out=junk[:],
+                        in_=words[:, e * 256 : (e + 1) * 256],
+                        func=ACT.Square,
+                        bias=neg_pad[:, 0:1],
+                        scale=1.0,
+                        accum_out=dist[:, g, e : e + 1],
+                    )
 
         def masked_identities(g):
             mid = mpool.tile([P, SLOTS, P], F32, name="mid", tag="mid")
             for e in range(SLOTS):
-                col = SLOTS * g + e
                 nc.vector.tensor_scalar(
-                    out=mid[:, e, :], in0=ident[:], scalar1=dist[:, col : col + 1], scalar2=0.0,
+                    out=mid[:, e, :], in0=perm[:], scalar1=dist[:, g, e : e + 1], scalar2=0.0,
                     op0=ALU.mult, op1=ALU.is_gt,
                 )
             return [mid[:, e, :] for e in range(SLOTS)]
@@ -149,7 +165,7 @@ def tile_linearnnencoder_kernel(tc, x, W, b, out):
             return y
 
         def statistics(g, ob, y):
-            yv = y[:].rearrange("o (e j r q) -> o j e q r", e=SLOTS, j=8, r=2, q=8)
+            yv = y[:].rearrange("o (e j m) -> o j e m", e=SLOTS, j=8, m=16)
             for j in range(8):
                 s0 = 16 * g + 2 * j
                 nc.vector.bn_stats(
@@ -172,6 +188,8 @@ def tile_linearnnencoder_kernel(tc, x, W, b, out):
         accs = {}
         pad_test(0, range(SLOTS))
         mids[0] = masked_identities(0)
+        for gv in V_TEST:
+            pad_test(gv, range(SLOTS))
         w_halves = transposes(w_sb, [ident[:]] * SLOTS)
         b_ps = psum_s.tile([P, OB], F32, name="b_ps", tag="misc")
         nc.tensor.matmul(out=b_ps[:], lhsT=b_rows[:], rhs=ident_bf[:], start=True, stop=True)
@@ -185,18 +203,14 @@ def tile_linearnnencoder_kernel(tc, x, W, b, out):
         grouped[0] = new_grouped()
         regroup(grouped[0], halves[0], 0, "scalar")
         regroup(grouped[0], halves[0], 1, "vector")
-        pad_test(1, range(SLOTS))
         x_q[0] = quantise(grouped[0])
         mids[1] = masked_identities(1)
         for ob in FIRST:
             accs[0, ob] = mx_pass(0, ob)
         halves[1] = transposes(x_sb[1], mids[1])
-        pad_test(2, [0, 1])
 
         for g in range(GROUPS):
             y0 = gelu(accs[g, FIRST[0]], FIRST[0])
-            if g == 0:
-                pad_test(2, [2, 3])
             if g + 1 < GROUPS:
                 grouped[g + 1] = new_grouped()
                 regroup(grouped[g + 1], halves[g + 1], 0, "scalar")
@@ -214,19 +228,19 @@ def tile_linearnnencoder_kernel(tc, x, W, b, out):
             if g + 2 < GROUPS:
                 halves[g + 2] = transposes(x_sb[g + 2], mids[g + 2])
             y1 = gelu(accs[g, FIRST[1]], FIRST[1])
-            if g + 3 < GROUPS:
+            if g + 3 < GROUPS and g + 3 not in V_TEST:
                 pad_test(g + 3, [0, 1])
             statistics(g, FIRST[1], y1)
             y2 = gelu(accs[g, FIRST[2]], FIRST[2])
-            if g + 3 < GROUPS:
+            if g + 3 < GROUPS and g + 3 not in V_TEST:
                 pad_test(g + 3, [2, 3])
             if g == GROUPS - 2:
-                valid = const.tile([P, GROUPS * SLOTS], F32, name="valid")
-                nc.vector.tensor_scalar(out=valid[:], in0=dist[:], scalar1=0.0, scalar2=None, op0=ALU.is_gt)
-                valid4 = const.tile([P, GROUPS], F32, name="valid4")
-                nc.vector.tensor_reduce(
-                    out=valid4[:], in_=valid[:].rearrange("p (g e) -> p g e", e=SLOTS), axis=AX.X, op=ALU.add
+                valid = const.tile([P, GROUPS, SLOTS], F32, name="valid")
+                nc.vector.tensor_scalar(
+                    out=valid[:], in0=dist[:, :, 0:SLOTS], scalar1=0.0, scalar2=None, op0=ALU.is_gt
                 )
+                valid4 = const.tile([P, GROUPS], F32, name="valid4")
+                nc.vector.tensor_reduce(out=valid4[:], in_=valid[:], axis=AX.X, op=ALU.add)
                 spread = const.tile([P, GROUPS, 16], BF16, name="spread")
                 nc.vector.tensor_tensor(
                     out=spread[:],
@@ -313,11 +327,14 @@ def tile_linearnnencoder_kernel(tc, x, W, b, out):
         accs[7, LAST] = mx_pass(7, LAST)
         statistics(5, LAST, gelu(accs[5, LAST], LAST))
         nc.scalar.activation(out=var[:, :nf], in_=m2v[:, :nf], func=ACT.Relu, scale=cinv[:, 0:1])
+        ctx.enter_context(tc.manual_schedule())
         statistics(6, LAST, gelu(accs[6, LAST], LAST))
         statistics(7, LAST, gelu(accs[7, LAST], LAST))
 
         warm2 = const.tile([P, 1], F32, name="warm2")
-        nc.scalar.activation(out=warm2[:], in_=stats[:, LAST, 16 * (GROUPS - 1), 0:1], func=ACT.Sqrt)
+        nc.scalar.activation(out=warm2[:], in_=ones_f[:], func=ACT.Sqrt)
+        nc.scalar.activation(out=res[:, :nf], in_=var[:, :nf], func=ACT.Sqrt)
+        nc.sync.dma_start(out=out[:, :nf], in_=res[:, :nf])
         c0 = LAST * P
         mean_l, m2_l = to_sample_rows([LAST])
         dl = fpool.tile([P, 512], F32, name="dl", tag="d")
@@ -338,5 +355,5 @@ def tile_linearnnencoder_kernel(tc, x, W, b, out):
             op1=ALU.add,
         )
         nc.sync.dma_start(out=out[:, OUT + c0 : OUT + c0 + P], in_=res[:, OUT + c0 : OUT + c0 + P])
-        nc.scalar.activation(out=res[:, :OUT], in_=var[:], func=ACT.Sqrt)
-        nc.sync.dma_start(out=out[:, :OUT], in_=res[:, :OUT])
+        nc.scalar.activation(out=res[:, c0 : c0 + P], in_=var[:, c0 : c0 + P], func=ACT.Sqrt)
+        nc.sync.dma_start(out=out[:, c0 : c0 + P], in_=res[:, c0 : c0 + P])

@@ -22,7 +22,7 @@ PAD_WORD = -(1.0 + 0xBF80 / 2.0**23)
 
 FIRST = [0, 1, 2]
 LAST = 3
-V_TEST = (1, 2, 3)
+V_COPY = (1, 3, 5, 7)
 
 
 def tile_linearnnencoder_kernel(tc, x, W, b, out):
@@ -76,44 +76,32 @@ def tile_linearnnencoder_kernel(tc, x, W, b, out):
         stats = const.tile([P, OB, SAMPLES, 3], F32, name="stats")
         res = const.tile([P, 2 * OUT], F32, name="res")
         var = const.tile([P, OUT], F32, name="var")
-        dist = const.tile([P, GROUPS, 8], F32, name="dist")
-        perm = const.tile([P, P], F32, name="perm")
-        nc.vector.tensor_copy(
-            out=perm[:].rearrange("p (j q r) -> p j q r", j=8, q=8, r=2),
-            in_=ident[:].rearrange("p (j r q) -> p j q r", j=8, r=2, q=8),
-        )
+        dist = const.tile([P, GROUPS * SLOTS], F32, name="dist")
 
         def pad_test(g, slots):
             words = x_sb[g][:].bitcast(F32)
             for e in slots:
-                if g in V_TEST:
-                    junkv = jpool.tile([P, 256], BF16, name="junkv", tag="junkv")
-                    nc.vector.tensor_scalar(
-                        out=junkv[:],
-                        in0=words[:, e * 256 : (e + 1) * 256],
-                        scalar1=PAD_WORD,
-                        scalar2=None,
-                        op0=ALU.not_equal,
-                        op1=ALU.add,
-                        accum_out=dist[:, g, e : e + 1],
-                    )
-                else:
-                    junk = jpool.tile([P, 256], BF16, name="junk", tag="junk")
-                    nc.scalar.activation(
-                        out=junk[:],
-                        in_=words[:, e * 256 : (e + 1) * 256],
-                        func=ACT.Square,
-                        bias=neg_pad[:, 0:1],
-                        scale=1.0,
-                        accum_out=dist[:, g, e : e + 1],
-                    )
+                junk = jpool.tile([P, 256], BF16, name="junk", tag="junk")
+                col = SLOTS * g + e
+                nc.scalar.activation(
+                    out=junk[:],
+                    in_=words[:, e * 256 : (e + 1) * 256],
+                    func=ACT.Square,
+                    bias=neg_pad[:, 0:1],
+                    scale=1.0,
+                    accum_out=dist[:, col : col + 1],
+                )
 
         def masked_identities(g):
             mid = mpool.tile([P, SLOTS, P], F32, name="mid", tag="mid")
+            ok = mpool.tile([P, SLOTS], F32, name="ok", tag="ok")
+            nc.gpsimd.tensor_scalar(
+                out=ok[:], in0=dist[:, SLOTS * g : SLOTS * (g + 1)], scalar1=0.0, scalar2=None, op0=ALU.is_gt
+            )
             for e in range(SLOTS):
-                nc.vector.tensor_scalar(
-                    out=mid[:, e, :], in0=perm[:], scalar1=dist[:, g, e : e + 1], scalar2=0.0,
-                    op0=ALU.mult, op1=ALU.is_gt,
+                nc.gpsimd.tensor_scalar(
+                    out=mid[:, e, :], in0=ident[:], scalar1=ok[:, e : e + 1], scalar2=0.0,
+                    op0=ALU.mult, op1=ALU.add,
                 )
             return [mid[:, e, :] for e in range(SLOTS)]
 
@@ -135,7 +123,7 @@ def tile_linearnnencoder_kernel(tc, x, W, b, out):
         def regroup(grouped, halves, h, engine):
             dst = grouped[:].bitcast(F32)[:, h * 512 : (h + 1) * 512].rearrange("k (e p u) -> k e p u", e=2, p=P, u=2)
             src = halves[h][:].rearrange("k e u p -> k e p u")
-            if engine in ("scalar", "vector"):
+            if engine == "scalar":
                 nc.scalar.copy(out=dst, in_=src)
             else:
                 nc.vector.tensor_copy(out=dst, in_=src)
@@ -165,7 +153,7 @@ def tile_linearnnencoder_kernel(tc, x, W, b, out):
             return y
 
         def statistics(g, ob, y):
-            yv = y[:].rearrange("o (e j m) -> o j e m", e=SLOTS, j=8, m=16)
+            yv = y[:].rearrange("o (e j r q) -> o j e q r", e=SLOTS, j=8, r=2, q=8)
             for j in range(8):
                 s0 = 16 * g + 2 * j
                 nc.vector.bn_stats(
@@ -188,8 +176,6 @@ def tile_linearnnencoder_kernel(tc, x, W, b, out):
         accs = {}
         pad_test(0, range(SLOTS))
         mids[0] = masked_identities(0)
-        for gv in V_TEST:
-            pad_test(gv, range(SLOTS))
         w_halves = transposes(w_sb, [ident[:]] * SLOTS)
         b_ps = psum_s.tile([P, OB], F32, name="b_ps", tag="misc")
         nc.tensor.matmul(out=b_ps[:], lhsT=b_rows[:], rhs=ident_bf[:], start=True, stop=True)
@@ -203,18 +189,22 @@ def tile_linearnnencoder_kernel(tc, x, W, b, out):
         grouped[0] = new_grouped()
         regroup(grouped[0], halves[0], 0, "scalar")
         regroup(grouped[0], halves[0], 1, "vector")
+        pad_test(1, range(SLOTS))
         x_q[0] = quantise(grouped[0])
         mids[1] = masked_identities(1)
         for ob in FIRST:
             accs[0, ob] = mx_pass(0, ob)
         halves[1] = transposes(x_sb[1], mids[1])
+        pad_test(2, [0, 1])
 
         for g in range(GROUPS):
             y0 = gelu(accs[g, FIRST[0]], FIRST[0])
+            if g == 0:
+                pad_test(2, [2, 3])
             if g + 1 < GROUPS:
                 grouped[g + 1] = new_grouped()
                 regroup(grouped[g + 1], halves[g + 1], 0, "scalar")
-                regroup(grouped[g + 1], halves[g + 1], 1, "vector")
+                regroup(grouped[g + 1], halves[g + 1], 1, "vector" if (g + 1) in V_COPY else "scalar")
             statistics(g, FIRST[0], y0)
             if g + 1 < GROUPS:
                 x_q[g + 1] = quantise(grouped[g + 1])
@@ -228,19 +218,19 @@ def tile_linearnnencoder_kernel(tc, x, W, b, out):
             if g + 2 < GROUPS:
                 halves[g + 2] = transposes(x_sb[g + 2], mids[g + 2])
             y1 = gelu(accs[g, FIRST[1]], FIRST[1])
-            if g + 3 < GROUPS and g + 3 not in V_TEST:
+            if g + 3 < GROUPS:
                 pad_test(g + 3, [0, 1])
             statistics(g, FIRST[1], y1)
             y2 = gelu(accs[g, FIRST[2]], FIRST[2])
-            if g + 3 < GROUPS and g + 3 not in V_TEST:
+            if g + 3 < GROUPS:
                 pad_test(g + 3, [2, 3])
             if g == GROUPS - 2:
-                valid = const.tile([P, GROUPS, SLOTS], F32, name="valid")
-                nc.vector.tensor_scalar(
-                    out=valid[:], in0=dist[:, :, 0:SLOTS], scalar1=0.0, scalar2=None, op0=ALU.is_gt
-                )
+                valid = const.tile([P, GROUPS * SLOTS], F32, name="valid")
+                nc.vector.tensor_scalar(out=valid[:], in0=dist[:], scalar1=0.0, scalar2=None, op0=ALU.is_gt)
                 valid4 = const.tile([P, GROUPS], F32, name="valid4")
-                nc.vector.tensor_reduce(out=valid4[:], in_=valid[:], axis=AX.X, op=ALU.add)
+                nc.vector.tensor_reduce(
+                    out=valid4[:], in_=valid[:].rearrange("p (g e) -> p g e", e=SLOTS), axis=AX.X, op=ALU.add
+                )
                 spread = const.tile([P, GROUPS, 16], BF16, name="spread")
                 nc.vector.tensor_tensor(
                     out=spread[:],
@@ -327,14 +317,11 @@ def tile_linearnnencoder_kernel(tc, x, W, b, out):
         accs[7, LAST] = mx_pass(7, LAST)
         statistics(5, LAST, gelu(accs[5, LAST], LAST))
         nc.scalar.activation(out=var[:, :nf], in_=m2v[:, :nf], func=ACT.Relu, scale=cinv[:, 0:1])
-        ctx.enter_context(tc.manual_schedule())
         statistics(6, LAST, gelu(accs[6, LAST], LAST))
         statistics(7, LAST, gelu(accs[7, LAST], LAST))
 
         warm2 = const.tile([P, 1], F32, name="warm2")
-        nc.scalar.activation(out=warm2[:], in_=ones_f[:], func=ACT.Sqrt)
-        nc.scalar.activation(out=res[:, :nf], in_=var[:, :nf], func=ACT.Sqrt)
-        nc.sync.dma_start(out=out[:, :nf], in_=res[:, :nf])
+        nc.scalar.activation(out=warm2[:], in_=stats[:, LAST, 16 * (GROUPS - 1), 0:1], func=ACT.Sqrt)
         c0 = LAST * P
         mean_l, m2_l = to_sample_rows([LAST])
         dl = fpool.tile([P, 512], F32, name="dl", tag="d")
@@ -355,5 +342,5 @@ def tile_linearnnencoder_kernel(tc, x, W, b, out):
             op1=ALU.add,
         )
         nc.sync.dma_start(out=out[:, OUT + c0 : OUT + c0 + P], in_=res[:, OUT + c0 : OUT + c0 + P])
-        nc.scalar.activation(out=res[:, c0 : c0 + P], in_=var[:, c0 : c0 + P], func=ACT.Sqrt)
-        nc.sync.dma_start(out=out[:, c0 : c0 + P], in_=res[:, c0 : c0 + P])
+        nc.scalar.activation(out=res[:, :OUT], in_=var[:], func=ACT.Sqrt)
+        nc.sync.dma_start(out=out[:, :OUT], in_=res[:, :OUT])

@@ -22,7 +22,7 @@ PAD_WORD = -(1.0 + 0xBF80 / 2.0**23)
 
 FIRST = [0, 1, 2]
 LAST = 3
-V_COPY = (1, 3, 5, 7)
+V_COPY = ()
 
 
 def tile_linearnnencoder_kernel(tc, x, W, b, out):
@@ -34,7 +34,7 @@ def tile_linearnnencoder_kernel(tc, x, W, b, out):
         cpool = ctx.enter_context(tc.tile_pool(name="cpool", bufs=GROUPS + 1))
         mpool = ctx.enter_context(tc.tile_pool(name="mpool", bufs=3))
         jpool = ctx.enter_context(tc.tile_pool(name="jpool", bufs=2))
-        ypool = ctx.enter_context(tc.tile_pool(name="ypool", bufs=6))
+        ypool = ctx.enter_context(tc.tile_pool(name="ypool", bufs=8))
         fpool = ctx.enter_context(tc.tile_pool(name="fpool", bufs=2))
         psum_t = ctx.enter_context(tc.psum_pool(name="psum_t", bufs=3))
         psum_a = ctx.enter_context(tc.psum_pool(name="psum_a", bufs=4))
@@ -76,33 +76,56 @@ def tile_linearnnencoder_kernel(tc, x, W, b, out):
         stats = const.tile([P, OB, SAMPLES, 3], F32, name="stats")
         res = const.tile([P, 2 * OUT], F32, name="res")
         var = const.tile([P, OUT], F32, name="var")
-        dist = const.tile([P, GROUPS * SLOTS], F32, name="dist")
+        dist = const.tile([P, GROUPS + 1, 8], F32, name="dist")
+
+        def dist_of(g, e):
+            if g == 0 and e >= 2:
+                return dist[:, GROUPS, e : e + 1]
+            return dist[:, g, e : e + 1]
 
         def pad_test(g, slots):
             words = x_sb[g][:].bitcast(F32)
             for e in slots:
-                junk = jpool.tile([P, 256], BF16, name="junk", tag="junk")
-                col = SLOTS * g + e
-                nc.scalar.activation(
-                    out=junk[:],
-                    in_=words[:, e * 256 : (e + 1) * 256],
-                    func=ACT.Square,
-                    bias=neg_pad[:, 0:1],
-                    scale=1.0,
-                    accum_out=dist[:, col : col + 1],
-                )
+                if g == 0 and e >= 2:
+                    junkv = jpool.tile([P, 256], BF16, name="junkv", tag="junkv")
+                    nc.vector.tensor_scalar(
+                        out=junkv[:],
+                        in0=words[:, e * 256 : (e + 1) * 256],
+                        scalar1=PAD_WORD,
+                        scalar2=None,
+                        op0=ALU.not_equal,
+                        op1=ALU.add,
+                        accum_out=dist_of(g, e),
+                    )
+                else:
+                    junk = jpool.tile([P, 256], BF16, name="junk", tag="junk")
+                    nc.scalar.activation(
+                        out=junk[:],
+                        in_=words[:, e * 256 : (e + 1) * 256],
+                        func=ACT.Square,
+                        bias=neg_pad[:, 0:1],
+                        scale=1.0,
+                        accum_out=dist_of(g, e),
+                    )
 
         def masked_identities(g):
             mid = mpool.tile([P, SLOTS, P], F32, name="mid", tag="mid")
-            ok = mpool.tile([P, SLOTS], F32, name="ok", tag="ok")
-            nc.gpsimd.tensor_scalar(
-                out=ok[:], in0=dist[:, SLOTS * g : SLOTS * (g + 1)], scalar1=0.0, scalar2=None, op0=ALU.is_gt
-            )
-            for e in range(SLOTS):
+            if g < 2:
+                for e in range(SLOTS):
+                    nc.vector.tensor_scalar(
+                        out=mid[:, e, :], in0=ident[:], scalar1=dist_of(g, e), scalar2=0.0,
+                        op0=ALU.mult, op1=ALU.is_gt,
+                    )
+            else:
+                ok = mpool.tile([P, SLOTS], F32, name="ok", tag="ok")
                 nc.gpsimd.tensor_scalar(
-                    out=mid[:, e, :], in0=ident[:], scalar1=ok[:, e : e + 1], scalar2=0.0,
-                    op0=ALU.mult, op1=ALU.add,
+                    out=ok[:], in0=dist[:, g, 0:SLOTS], scalar1=0.0, scalar2=None, op0=ALU.is_gt
                 )
+                for e in range(SLOTS):
+                    nc.gpsimd.tensor_scalar(
+                        out=mid[:, e, :], in0=ident[:], scalar1=ok[:, e : e + 1], scalar2=0.0,
+                        op0=ALU.mult, op1=ALU.add,
+                    )
             return [mid[:, e, :] for e in range(SLOTS)]
 
         def transposes(src, idents):
@@ -225,12 +248,18 @@ def tile_linearnnencoder_kernel(tc, x, W, b, out):
             if g + 3 < GROUPS:
                 pad_test(g + 3, [2, 3])
             if g == GROUPS - 2:
-                valid = const.tile([P, GROUPS * SLOTS], F32, name="valid")
-                nc.vector.tensor_scalar(out=valid[:], in0=dist[:], scalar1=0.0, scalar2=None, op0=ALU.is_gt)
-                valid4 = const.tile([P, GROUPS], F32, name="valid4")
-                nc.vector.tensor_reduce(
-                    out=valid4[:], in_=valid[:].rearrange("p (g e) -> p g e", e=SLOTS), axis=AX.X, op=ALU.add
+                valid = const.tile([P, GROUPS, SLOTS], F32, name="valid")
+                nc.vector.tensor_scalar(
+                    out=valid[:, 1:, :], in0=dist[:, 1:GROUPS, 0:SLOTS], scalar1=0.0, scalar2=None, op0=ALU.is_gt
                 )
+                nc.vector.tensor_scalar(
+                    out=valid[:, 0, 0:2], in0=dist[:, 0, 0:2], scalar1=0.0, scalar2=None, op0=ALU.is_gt
+                )
+                nc.vector.tensor_scalar(
+                    out=valid[:, 0, 2:4], in0=dist[:, GROUPS, 2:4], scalar1=0.0, scalar2=None, op0=ALU.is_gt
+                )
+                valid4 = const.tile([P, GROUPS], F32, name="valid4")
+                nc.vector.tensor_reduce(out=valid4[:], in_=valid[:], axis=AX.X, op=ALU.add)
                 spread = const.tile([P, GROUPS, 16], BF16, name="spread")
                 nc.vector.tensor_tensor(
                     out=spread[:],
@@ -291,7 +320,7 @@ def tile_linearnnencoder_kernel(tc, x, W, b, out):
             )
         statistics(1, LAST, gelu(accs[1, LAST], LAST))
         ypad_nz = const.tile([P, OUT], F32, name="ypad_nz")
-        nc.vector.tensor_scalar(out=ypad_nz[:], in0=ypad_bc[:], scalar1=nz[:, 0:1], scalar2=None, op0=ALU.mult)
+        nc.scalar.activation(out=ypad_nz[:], in_=ypad_bc[:], func=ACT.Copy, scale=nz[:, 0:1])
         accs[4, LAST] = mx_pass(4, LAST)
         statistics(2, LAST, gelu(accs[2, LAST], LAST))
 

@@ -22,7 +22,7 @@ PAD_WORD = -(1.0 + 0xBF80 / 2.0**23)
 
 FIRST = [0, 1, 2]
 LAST = 3
-V_COPY = ()
+V_COPY = (3, 6)
 
 
 def tile_linearnnencoder_kernel(tc, x, W, b, out):
@@ -110,7 +110,7 @@ def tile_linearnnencoder_kernel(tc, x, W, b, out):
 
         def masked_identities(g):
             mid = mpool.tile([P, SLOTS, P], F32, name="mid", tag="mid")
-            if g < 2:
+            if g < GROUPS:
                 for e in range(SLOTS):
                     nc.vector.tensor_scalar(
                         out=mid[:, e, :], in0=ident[:], scalar1=dist_of(g, e), scalar2=0.0,

@@ -346,11 +346,14 @@ def tile_linearnnencoder_kernel(tc, x, W, b, out):
         accs[7, LAST] = mx_pass(7, LAST)
         statistics(5, LAST, gelu(accs[5, LAST], LAST))
         nc.scalar.activation(out=var[:, :nf], in_=m2v[:, :nf], func=ACT.Relu, scale=cinv[:, 0:1])
+        ctx.enter_context(tc.manual_schedule())
         statistics(6, LAST, gelu(accs[6, LAST], LAST))
         statistics(7, LAST, gelu(accs[7, LAST], LAST))
 
         warm2 = const.tile([P, 1], F32, name="warm2")
-        nc.scalar.activation(out=warm2[:], in_=stats[:, LAST, 16 * (GROUPS - 1), 0:1], func=ACT.Sqrt)
+        nc.scalar.activation(out=warm2[:], in_=ones_f[:], func=ACT.Sqrt)
+        nc.scalar.activation(out=res[:, :nf], in_=var[:, :nf], func=ACT.Sqrt)
+        nc.sync.dma_start(out=out[:, :nf], in_=res[:, :nf])
         c0 = LAST * P
         mean_l, m2_l = to_sample_rows([LAST])
         dl = fpool.tile([P, 512], F32, name="dl", tag="d")
@@ -371,5 +374,5 @@ def tile_linearnnencoder_kernel(tc, x, W, b, out):
             op1=ALU.add,
         )
         nc.sync.dma_start(out=out[:, OUT + c0 : OUT + c0 + P], in_=res[:, OUT + c0 : OUT + c0 + P])
-        nc.scalar.activation(out=res[:, :OUT], in_=var[:], func=ACT.Sqrt)
-        nc.sync.dma_start(out=out[:, :OUT], in_=res[:, :OUT])
+        nc.scalar.activation(out=res[:, c0 : c0 + P], in_=var[:, c0 : c0 + P], func=ACT.Sqrt)
+        nc.sync.dma_start(out=out[:, c0 : c0 + P], in_=res[:, c0 : c0 + P])

from contextlib import ExitStack

import concourse.mybir as mybir
from concourse.masks import make_identity

FP8X4 = mybir.dt.float8_e4m3fn_x4
F32 = mybir.dt.float32
BF16 = mybir.dt.bfloat16
U32 = mybir.dt.uint32
U8 = mybir.dt.uint8
ACT = mybir.ActivationFunctionType
ALU = mybir.AluOpType
AX = mybir.AxisListType

P = 128
SAMPLES, TOKENS, K, OUT = 128, 32, 512, 512
GROUPS = 8
SLOTS = 4
OB = OUT // P
FLOPS = 2 * SAMPLES * TOKENS * K * OUT
PAD_WORD = -(1.0 + 0xBF80 / 2.0**23)

FIRST = [0, 1, 2]
LAST = 3
V_COPY = (3, 6)


def tile_linearnnencoder_kernel(tc, x, W, b, out):
    nc = tc.nc
    with ExitStack() as ctx:
        const = ctx.enter_context(tc.tile_pool(name="const", bufs=1))
        xpool = ctx.enter_context(tc.tile_pool(name="xpool", bufs=GROUPS))
        gpool = ctx.enter_context(tc.tile_pool(name="gpool", bufs=2))
        cpool = ctx.enter_context(tc.tile_pool(name="cpool", bufs=GROUPS + 1))
        mpool = ctx.enter_context(tc.tile_pool(name="mpool", bufs=3))
        jpool = ctx.enter_context(tc.tile_pool(name="jpool", bufs=2))
        ypool = ctx.enter_context(tc.tile_pool(name="ypool", bufs=8))
        fpool = ctx.enter_context(tc.tile_pool(name="fpool", bufs=2))
        psum_t = ctx.enter_context(tc.psum_pool(name="psum_t", bufs=3))
        psum_a = ctx.enter_context(tc.psum_pool(name="psum_a", bufs=4))
        psum_s = ctx.enter_context(tc.psum_pool(name="psum_s", bufs=1))

        b_rows = const.tile([P, P], BF16, name="b_rows")
        nc.vector.memset(b_rows[:], 0.0)
        nc.scalar.dma_start(out=b_rows[0:OB, :], in_=b.rearrange("(ob o) -> ob o", ob=OB))
        x_groups = x.flatten_outer_dims().rearrange("(g p e) k -> g p (e k)", g=GROUPS, p=P, e=SLOTS)
        x_sb = []
        w_sb = const.tile([P, SLOTS * K], BF16, name="w_sb")
        for g in range(GROUPS):
            xin = xpool.tile([P, SLOTS * K], BF16, name="xin", tag="xin")
            nc.sync.dma_start(out=xin[:], in_=x_groups[g])
            x_sb.append(xin)
            if g == 0:
                nc.sync.dma_start(
                    out=w_sb[:].rearrange("p (ob k) -> p ob k", ob=OB),
                    in_=W.rearrange("(ob p) k -> p ob k", p=P),
                )

        ident = const.tile([P, P], F32, name="ident")
        make_identity(nc, ident[:])
        ones_f = const.tile([P, 1], F32, name="ones_f")
        nc.vector.memset(ones_f[:], 1.0)
        warm = const.tile([P, 1], F32, name="warm")
        nc.scalar.activation(out=warm[:], in_=ones_f[:], func=ACT.Gelu)
        neg_pad = const.tile([P, 1], F32, name="neg_pad")
        nc.vector.memset(neg_pad[:], -PAD_WORD)
        ones_bf = const.tile([P, 2], BF16, name="ones_bf")
        nc.vector.memset(ones_bf[:], 1.0)
        ident_bf = const.tile([P, OB], BF16, name="ident_bf")
        nc.vector.tensor_copy(out=ident_bf[:], in_=ident[:, 0:OB])
        group_of = const.tile([P, 16], F32, name="group_of")
        nc.vector.tensor_reduce(
            out=group_of[:], in_=ident[:].rearrange("p (s q) -> p s q", q=8), axis=AX.X, op=ALU.add
        )

        stats = const.tile([P, OB, SAMPLES, 3], F32, name="stats")
        res = const.tile([P, 2 * OUT], F32, name="res")
        var = const.tile([P, OUT], F32, name="var")
        dist = const.tile([P, GROUPS + 1, 8], F32, name="dist")

        def dist_of(g, e):
            if g == 0 and e >= 2:
                return dist[:, GROUPS, e : e + 1]
            return dist[:, g, e : e + 1]

        def pad_test(g, slots):
            words = x_sb[g][:].bitcast(F32)
            for e in slots:
                if g == 0 and e >= 2:
                    junkv = jpool.tile([P, 256], BF16, name="junkv", tag="junkv")
                    nc.vector.tensor_scalar(
                        out=junkv[:],
                        in0=words[:, e * 256 : (e + 1) * 256],
                        scalar1=PAD_WORD,
                        scalar2=None,
                        op0=ALU.not_equal,
                        op1=ALU.add,
                        accum_out=dist_of(g, e),
                    )
                else:
                    junk = jpool.tile([P, 256], BF16, name="junk", tag="junk")
                    nc.scalar.activation(
                        out=junk[:],
                        in_=words[:, e * 256 : (e + 1) * 256],
                        func=ACT.Square,
                        bias=neg_pad[:, 0:1],
                        scale=1.0,
                        accum_out=dist_of(g, e),
                    )

        def masked_identities(g):
            mid = mpool.tile([P, SLOTS, P], F32, name="mid", tag="mid")
            if g < GROUPS:
                for e in range(SLOTS):
                    nc.vector.tensor_scalar(
                        out=mid[:, e, :], in0=ident[:], scalar1=dist_of(g, e), scalar2=0.0,
                        op0=ALU.mult, op1=ALU.is_gt,
                    )
            else:
                ok = mpool.tile([P, SLOTS], F32, name="ok", tag="ok")
                nc.gpsimd.tensor_scalar(
                    out=ok[:], in0=dist[:, g, 0:SLOTS], scalar1=0.0, scalar2=None, op0=ALU.is_gt
                )
                for e in range(SLOTS):
                    nc.gpsimd.tensor_scalar(
                        out=mid[:, e, :], in0=ident[:], scalar1=ok[:, e : e + 1], scalar2=0.0,
                        op0=ALU.mult, op1=ALU.add,
                    )
            return [mid[:, e, :] for e in range(SLOTS)]

        def transposes(src, idents):
            words = src[:].bitcast(F32)
            halves = []
            for h in range(2):
                xt = psum_t.tile([P, 2, 2, P], F32, name="xt", tag="xt")
                for e2 in range(2):
                    for u in range(2):
                        c0 = (2 * h + e2) * 256 + u * P
                        nc.tensor.transpose(xt[:, e2, u, :], words[:, c0 : c0 + P], idents[2 * h + e2])
                halves.append(xt)
            return halves

        def new_grouped():
            return gpool.tile([P, SLOTS * K], BF16, name="grouped", tag="grouped", align_bytes=64)

        def regroup(grouped, halves, h, engine):
            dst = grouped[:].bitcast(F32)[:, h * 512 : (h + 1) * 512].rearrange("k (e p u) -> k e p u", e=2, p=P, u=2)
            src = halves[h][:].rearrange("k e u p -> k e p u")
            if engine == "scalar":
                nc.scalar.copy(out=dst, in_=src)
            else:
                nc.vector.tensor_copy(out=dst, in_=src)

        def quantise(grouped):
            codes = cpool.tile([P, 512], U32, name="codes", tag="codes", align_bytes=64)
            scales = cpool.tile([P, 512], U8, name="scales", tag="scales", align_bytes=64)
            nc.vector.quantize_mx(out=codes[:].bitcast(FP8X4), scales=scales[:], in_=grouped[:])
            return codes, scales

        def mx_pass(g, ob):
            acc = psum_a.tile([P, 512], F32, name="acc", tag="acc")
            nc.tensor.matmul_mx(
                out=acc[:],
                lhsT=w_codes[:, ob * P : (ob + 1) * P].bitcast(FP8X4),
                lhsT_scale=w_scales[:, ob * P : (ob + 1) * P],
                rhs=x_q[g][0][:].bitcast(FP8X4),
                rhs_scale=x_q[g][1][:],
                start=True,
                stop=True,
            )
            return acc

        def gelu(acc, ob):
            y = ypool.tile([P, 512], F32, name="y", tag="y")
            nc.scalar.activation(out=y[:], in_=acc[:], func=ACT.Gelu, bias=b_col[:, ob : ob + 1], scale=1.0)
            return y

        def statistics(g, ob, y):
            yv = y[:].rearrange("o (e j r q) -> o j e q r", e=SLOTS, j=8, r=2, q=8)
            for j in range(8):
                s0 = 16 * g + 2 * j
                nc.vector.bn_stats(
                    out=stats[:, ob, s0 : s0 + 2, :].rearrange("o s c -> o (s c)"), in_=yv[:, j]
                )

        def to_sample_rows(blocks):
            mean_t = psum_t.tile([P, 512], F32, name="mean_t", tag="xt")
            m2_t = psum_t.tile([P, 512], F32, name="m2_t", tag="xt")
            for i, ob in enumerate(blocks):
                nc.tensor.transpose(mean_t[:, i * P : (i + 1) * P], stats[:, ob, :, 1], ident[:])
            for i, ob in enumerate(blocks):
                nc.tensor.transpose(m2_t[:, i * P : (i + 1) * P], stats[:, ob, :, 2], ident[:])
            return mean_t, m2_t

        mids = {}
        halves = {}
        grouped = {}
        x_q = {}
        accs = {}
        pad_test(0, range(SLOTS))
        mids[0] = masked_identities(0)
        w_halves = transposes(w_sb, [ident[:]] * SLOTS)
        b_ps = psum_s.tile([P, OB], F32, name="b_ps", tag="misc")
        nc.tensor.matmul(out=b_ps[:], lhsT=b_rows[:], rhs=ident_bf[:], start=True, stop=True)
        w_grouped = new_grouped()
        regroup(w_grouped, w_halves, 0, "scalar")
        regroup(w_grouped, w_halves, 1, "vector")
        halves[0] = transposes(x_sb[0], mids[0])
        w_codes, w_scales = quantise(w_grouped)
        b_col = const.tile([P, OB], F32, name="b_col")
        nc.vector.tensor_copy(out=b_col[:], in_=b_ps[:])
        grouped[0] = new_grouped()
        regroup(grouped[0], halves[0], 0, "scalar")
        regroup(grouped[0], halves[0], 1, "vector")
        pad_test(1, range(SLOTS))
        x_q[0] = quantise(grouped[0])
        mids[1] = masked_identities(1)
        for ob in FIRST:
            accs[0, ob] = mx_pass(0, ob)
        halves[1] = transposes(x_sb[1], mids[1])
        pad_test(2, [0, 1])

        for g in range(GROUPS):
            y0 = gelu(accs[g, FIRST[0]], FIRST[0])
            if g == 0:
                pad_test(2, [2, 3])
            if g + 1 < GROUPS:
                grouped[g + 1] = new_grouped()
                regroup(grouped[g + 1], halves[g + 1], 0, "scalar")
                regroup(grouped[g + 1], halves[g + 1], 1, "vector" if (g + 1) in V_COPY else "scalar")
            statistics(g, FIRST[0], y0)
            if g + 1 < GROUPS:
                x_q[g + 1] = quantise(grouped[g + 1])
            if g + 2 < GROUPS:
                mids[g + 2] = masked_identities(g + 2)
            if g + 1 < GROUPS:
                for ob in FIRST:
                    accs[g + 1, ob] = mx_pass(g + 1, ob)
            else:
                accs[0, LAST] = mx_pass(0, LAST)
            if g + 2 < GROUPS:
                halves[g + 2] = transposes(x_sb[g + 2], mids[g + 2])
            y1 = gelu(accs[g, FIRST[1]], FIRST[1])
            if g + 3 < GROUPS:
                pad_test(g + 3, [0, 1])
            statistics(g, FIRST[1], y1)
            y2 = gelu(accs[g, FIRST[2]], FIRST[2])
            if g + 3 < GROUPS:
                pad_test(g + 3, [2, 3])
            if g == GROUPS - 2:
                valid = const.tile([P, GROUPS, SLOTS], F32, name="valid")
                nc.vector.tensor_scalar(
                    out=valid[:, 1:, :], in0=dist[:, 1:GROUPS, 0:SLOTS], scalar1=0.0, scalar2=None, op0=ALU.is_gt
                )
                nc.vector.tensor_scalar(
                    out=valid[:, 0, 0:2], in0=dist[:, 0, 0:2], scalar1=0.0, scalar2=None, op0=ALU.is_gt
                )
                nc.vector.tensor_scalar(
                    out=valid[:, 0, 2:4], in0=dist[:, GROUPS, 2:4], scalar1=0.0, scalar2=None, op0=ALU.is_gt
                )
                valid4 = const.tile([P, GROUPS], F32, name="valid4")
                nc.vector.tensor_reduce(out=valid4[:], in_=valid[:], axis=AX.X, op=ALU.add)
                spread = const.tile([P, GROUPS, 16], BF16, name="spread")
                nc.vector.tensor_tensor(
                    out=spread[:],
                    in0=valid4[:].unsqueeze(2).to_broadcast([P, GROUPS, 16]),
                    in1=group_of[:].unsqueeze(1).to_broadcast([P, GROUPS, 16]),
                    op=ALU.mult,
                )
                nv_ps = psum_s.tile([P, 1], F32, name="nv_ps", tag="misc")
                nc.tensor.matmul(
                    out=nv_ps[:], lhsT=spread[:].rearrange("p g s -> p (g s)"), rhs=ones_bf[:, 0:1],
                    start=True, stop=True,
                )
            statistics(g, FIRST[2], y2)

        nval = const.tile([P, 1], F32, name="nval")
        nc.vector.tensor_copy(out=nval[:], in_=nv_ps[:])
        npad = const.tile([P, 1], F32, name="npad")
        nc.vector.tensor_scalar(
            out=npad[:], in0=nval[:], scalar1=-1.0, scalar2=float(TOKENS), op0=ALU.mult, op1=ALU.add
        )
        nmax = const.tile([P, 1], F32, name="nmax")
        nc.vector.tensor_scalar_max(out=nmax[:], in0=nval[:], scalar1=1.0)
        rn = const.tile([P, 1], F32, name="rn")
        nc.vector.reciprocal(out=rn[:], in_=nmax[:])
        nz = const.tile([P, 1], F32, name="nz")
        nc.vector.tensor_scalar_min(out=nz[:], in0=nval[:], scalar1=1.0)
        a2 = const.tile([P, 1], F32, name="a2")
        nc.vector.tensor_scalar(
            out=a2[:], in0=rn[:], scalar1=nz[:, 0:1], scalar2=float(TOKENS), op0=ALU.mult, op1=ALU.mult
        )
        rneg = const.tile([P, 1], F32, name="rneg")
        nc.vector.tensor_scalar(
            out=rneg[:], in0=npad[:], scalar1=rn[:, 0:1], scalar2=-float(TOKENS), op0=ALU.mult, op1=ALU.mult
        )
        n1 = const.tile([P, 1], F32, name="n1")
        nc.vector.tensor_scalar(out=n1[:], in0=nval[:], scalar1=-1.0, scalar2=1.0, op0=ALU.add, op1=ALU.max)
        rn1 = const.tile([P, 1], F32, name="rn1")
        nc.vector.reciprocal(out=rn1[:], in_=n1[:])
        cinv = const.tile([P, 1], F32, name="cinv")
        nc.vector.tensor_scalar(
            out=cinv[:], in0=nval[:], scalar1=1.0, scalar2=rn1[:, 0:1], op0=ALU.is_gt, op1=ALU.mult
        )

        for g in (1, 2, 3):
            accs[g, LAST] = mx_pass(g, LAST)
        y = gelu(accs[0, LAST], LAST)
        ypad = const.tile([P, OB], F32, name="ypad")
        nc.scalar.activation(out=ypad[:], in_=b_col[:], func=ACT.Gelu)
        statistics(0, LAST, y)
        ypad_bc = psum_t.tile([P, OUT], F32, name="ypad_bc", tag="xt")
        for ob in range(OB):
            nc.tensor.matmul(
                out=ypad_bc[:, ob * P : (ob + 1) * P],
                lhsT=ypad[:, ob : ob + 1].to_broadcast([P, P]),
                rhs=ident[:],
                start=True,
                stop=True,
            )
        statistics(1, LAST, gelu(accs[1, LAST], LAST))
        ypad_nz = const.tile([P, OUT], F32, name="ypad_nz")
        nc.scalar.activation(out=ypad_nz[:], in_=ypad_bc[:], func=ACT.Copy, scale=nz[:, 0:1])
        accs[4, LAST] = mx_pass(4, LAST)
        statistics(2, LAST, gelu(accs[2, LAST], LAST))

        nf = len(FIRST) * P
        mean_t, m2_t = to_sample_rows(FIRST)
        accs[5, LAST] = mx_pass(5, LAST)
        d = fpool.tile([P, 512], F32, name="d", tag="d")
        nc.vector.tensor_tensor(out=d[:, :nf], in0=mean_t[:, :nf], in1=ypad_nz[:, :nf], op=ALU.subtract)
        nc.vector.scalar_tensor_tensor(
            out=res[:, OUT : OUT + nf], in0=d[:, :nf], scalar=a2[:, 0:1], in1=ypad_nz[:, :nf], op0=ALU.mult, op1=ALU.add
        )
        nc.sync.dma_start(out=out[:, OUT : OUT + nf], in_=res[:, OUT : OUT + nf])
        y3 = gelu(accs[3, LAST], LAST)
        dd = fpool.tile([P, 512], F32, name="dd", tag="dd")
        nc.scalar.activation(out=dd[:, :nf], in_=d[:, :nf], func=ACT.Square)
        statistics(3, LAST, y3)
        m2v = fpool.tile([P, 512], F32, name="m2v", tag="m2v")
        nc.vector.scalar_tensor_tensor(
            out=m2v[:, :nf], in0=dd[:, :nf], scalar=rneg[:, 0:1], in1=m2_t[:, :nf], op0=ALU.mult, op1=ALU.add
        )
        accs[6, LAST] = mx_pass(6, LAST)
        statistics(4, LAST, gelu(accs[4, LAST], LAST))
        accs[7, LAST] = mx_pass(7, LAST)
        statistics(5, LAST, gelu(accs[5, LAST], LAST))
        nc.scalar.activation(out=var[:, :nf], in_=m2v[:, :nf], func=ACT.Relu, scale=cinv[:, 0:1])
        ctx.enter_context(tc.manual_schedule())
        statistics(6, LAST, gelu(accs[6, LAST], LAST))
        statistics(7, LAST, gelu(accs[7, LAST], LAST))

        warm2 = const.tile([P, 1], F32, name="warm2")
        nc.scalar.activation(out=warm2[:], in_=ones_f[:], func=ACT.Sqrt)
        nc.scalar.activation(out=res[:, :nf], in_=var[:, :nf], func=ACT.Sqrt)
        nc.sync.dma_start(out=out[:, :nf], in_=res[:, :nf])
        c0 = LAST * P
        mean_l, m2_l = to_sample_rows([LAST])
        dl = fpool.tile([P, 512], F32, name="dl", tag="d")
        nc.vector.tensor_tensor(out=dl[:, :P], in0=mean_l[:, :P], in1=ypad_nz[:, c0 : c0 + P], op=ALU.subtract)
        ddl = fpool.tile([P, 512], F32, name="ddl", tag="dd")
        nc.vector.scalar_tensor_tensor(
            out=ddl[:, :P], in0=dl[:, :P], scalar=rneg[:, 0:1], in1=dl[:, :P], op0=ALU.mult, op1=ALU.mult
        )
        m2l = fpool.tile([P, 512], F32, name="m2l", tag="m2v")
        nc.vector.tensor_tensor(out=m2l[:, :P], in0=m2_l[:, :P], in1=ddl[:, :P], op=ALU.add)
        nc.scalar.activation(out=var[:, c0 : c0 + P], in_=m2l[:, :P], func=ACT.Relu, scale=cinv[:, 0:1])
        nc.vector.scalar_tensor_tensor(
            out=res[:, OUT + c0 : OUT + c0 + P],
            in0=dl[:, :P],
            scalar=a2[:, 0:1],
            in1=ypad_nz[:, c0 : c0 + P],
            op0=ALU.mult,
            op1=ALU.add,
        )
        nc.sync.dma_start(out=out[:, OUT + c0 : OUT + c0 + P], in_=res[:, OUT + c0 : OUT + c0 + P])
        nc.scalar.activation(out=res[:, c0 : c0 + P], in_=var[:, c0 : c0 + P], func=ACT.Sqrt)
        nc.sync.dma_start(out=out[:, c0 : c0 + P], in_=res[:, c0 : c0 + P])
